import numpy as np
import ml_dtypes


def mxq(x, axis, fmt="e4m3"):
    dtype, down = {"e4m3": (ml_dtypes.float8_e4m3fn, 7), "e5m2": (ml_dtypes.float8_e5m2, 14)}[fmt]
    v = np.moveaxis(np.asarray(x, np.float32).astype(ml_dtypes.bfloat16).astype(np.float64), axis, -1)
    blocks = v.reshape(v.shape[:-1] + (-1, 32))
    amax = np.abs(blocks).max(-1, keepdims=True)
    byte = np.maximum(np.where(amax > 0, np.frexp(amax)[1] - 1 + 127, 0) - down, 1)
    scale = np.exp2(byte - 127.0)
    codes = (blocks / scale).astype(np.float32).astype(dtype).astype(np.float64)
    return np.moveaxis((codes * scale).reshape(v.shape), -1, axis)


WIDE = False


def mx_kscale(k):
    if not WIDE:
        return np.ones(k)
    levels = np.array([10, -10, 5, -5, 0])
    a = np.random.permutation(np.resize(levels, k // 512 * 4)).reshape(k // 512, 4)
    idx = np.arange(k)
    return np.exp2(a[idx // 512, idx % 128 // 32])


BF16 = ml_dtypes.bfloat16


def bf(x):
    return np.asarray(x, np.float32).astype(BF16)


def f64(x):
    return np.asarray(x).astype(np.float64)


B, T, I, H = 128, 32, 1024, 256


def sigmoid(v):
    return 1.0 / (1.0 + np.exp(-v))


def setup_inputs():
    s = mx_kscale(I)
    d = {"x": bf(np.random.standard_normal((B, T, I)) * s),
         "h0": bf(np.random.standard_normal((B, H))),
         "c0": bf(np.random.standard_normal((B, H)))}
    for n in ("f", "i", "g"):
        d["W_" + n] = bf(np.random.standard_normal((H, I)) / np.sqrt(I) / s)
        d["b_" + n] = bf(np.random.standard_normal(H) * 0.5)
        d["R_" + n] = bf(np.random.standard_normal((H, H)) / np.sqrt(H))
        d["rb_" + n] = bf(np.random.standard_normal(H) * 0.5)
    return d


def reference(x, h0, c0, W_f, b_f, R_f, rb_f, W_i, b_i, R_i, rb_i, W_g, b_g, R_g, rb_g):
    xq = mxq(f64(x), 2, "e4m3")
    h0v = f64(h0)

    def pre(W, b, R, rb):
        return (xq @ mxq(f64(W), 1, "e4m3").T) + f64(b) + (h0v @ f64(R).T + f64(rb))[:, None, :]

    ft = sigmoid(pre(W_f, b_f, R_f, rb_f))
    it = sigmoid(pre(W_i, b_i, R_i, rb_i))
    gt = np.tanh(pre(W_g, b_g, R_g, rb_g))
    c = ft * f64(c0)[:, None, :] + it * gt
    h_seq = np.tanh(c)
    hidden_seq = np.transpose(h_seq, (1, 0, 2)).reshape(T * B, H).T
    return (hidden_seq, h_seq[:, -1, :], c[:, -1, :])

@@ -1,0 +1,287 @@
+from contextlib import ExitStack
+
+import concourse.mybir as mybir
+from concourse.masks import make_identity
+
+F32 = mybir.dt.float32
+BF16 = mybir.dt.bfloat16
+U32 = mybir.dt.uint32
+U8 = mybir.dt.uint8
+FP8X4 = mybir.dt.float8_e4m3fn_x4
+ACT = mybir.ActivationFunctionType
+ALU = mybir.AluOpType
+
+P = 128
+B, T, I, H = 128, 32, 1024, 256
+GATES = 3
+G_GATE, I_GATE, F_GATE = 0, 1, 2
+GATE_FUNC = (ACT.Tanh, ACT.Sigmoid, ACT.Sigmoid)
+PACK = 4
+K_PASS = P * PACK
+PASSES = I // K_PASS
+WORDS = I // 2
+PLANES = WORDS // P
+H_HALVES = H // P
+T_CHUNK = 4
+N = T_CHUNK * B
+CHUNKS = T // T_CHUNK
+UNITS = CHUNKS * H_HALVES
+
+ACT_LAG = 1
+CELL_LAG = 2
+OUT_LAG = 3
+LAST_LAG = 5
+
+FLOPS = 2 * B * T * I * GATES * H + 2 * B * H * GATES * H
+
+
+def block_to_grouped(nc, psum, src_words, ident_f32, grouped, cols, first_col, on_vector):
+    planes = psum.tile([P, PLANES, P], F32, name="planes", tag="xt")
+    for q in range(PLANES):
+        nc.tensor.transpose(planes[:, q, :], src_words[:, q * P : (q + 1) * P], ident_f32)
+    grouped_words = grouped.bitcast(F32).rearrange("p (g c u) -> p g c u", g=PASSES, c=cols)
+    dst = grouped_words[:, :, first_col : first_col + P, :]
+    src = planes[:].rearrange("p (g u) c -> p g c u", g=PASSES)
+    if on_vector:
+        nc.vector.tensor_copy(out=dst, in_=src)
+    else:
+        nc.scalar.copy(out=dst, in_=src)
+
+
+def tile_lstm_cell_pa_t_kernel(
+    tc, x, h0, c0, W_f, b_f, R_f, rb_f, W_i, b_i, R_i, rb_i, W_g, b_g, R_g, rb_g, out_0, out_1, out_2
+):
+    nc = tc.nc
+    w_dram = (W_g, W_i, W_f)
+    r_dram = (R_g, R_i, R_f)
+    bias_dram = (b_g, rb_g, b_i, rb_i, b_f, rb_f)
+    order = list(reversed(range(CHUNKS)))
+
+    with ExitStack() as ctx:
+        ctx.enter_context(tc.manual_schedule())
+        keep = ctx.enter_context(tc.tile_pool(name="keep", bufs=1))
+        stage = ctx.enter_context(tc.tile_pool(name="stage", bufs=2))
+        work = ctx.enter_context(tc.tile_pool(name="work", bufs=4))
+        psum = ctx.enter_context(tc.psum_pool(name="psum", bufs=4))
+
+        h0_sb = keep.tile([P, H], BF16, name="h0_sb")
+        nc.sync.dma_start(out=h0_sb[:], in_=h0)
+        c0_sb = keep.tile([P, H], BF16, name="c0_sb")
+        nc.sync.dma_start(out=c0_sb[:], in_=c0)
+        r_sb = keep.tile([P, GATES, H_HALVES, H], BF16, name="r_sb")
+        for n in range(GATES):
+            nc.sync.dma_start(out=r_sb[:, n, :, :], in_=r_dram[n].rearrange("(h j) k -> j h k", j=P))
+        w_sb = keep.tile([P, H_HALVES, GATES, I], BF16, name="w_sb")
+        x_sb = []
+        for k in range(CHUNKS):
+            x_sb.append(keep.tile([P, T_CHUNK * I], BF16, name="x_sb%d" % k))
+
+        def load_w(jh):
+            for n in range(GATES):
+                nc.sync.dma_start(out=w_sb[:, jh, n, :], in_=w_dram[n][jh * P : (jh + 1) * P, :])
+
+        def load_x(k):
+            for half in range(2):
+                t0 = order[k] * T_CHUNK + half * 2
+                nc.sync.dma_start(
+                    out=x_sb[k][:, half * 2 * I : (half + 1) * 2 * I],
+                    in_=x[:, t0 : t0 + 2, :].rearrange("b t k -> b (t k)"),
+                )
+
+        load_w(0)
+        load_x(0)
+        load_w(1)
+        for k in range(1, CHUNKS):
+            load_x(k)
+
+        ident_bf16 = keep.tile([P, P], BF16, name="ident_bf16")
+        make_identity(nc, ident_bf16[:])
+        ident_f32 = keep.tile([P, P], F32, name="ident_f32")
+        nc.vector.tensor_copy(out=ident_f32[:], in_=ident_bf16[:])
+        bias_rows = keep.tile([P, H], BF16, name="bias_rows")
+        nc.vector.memset(bias_rows[:], 0.0)
+        for row in range(2 * GATES):
+            nc.gpsimd.dma_start(out=bias_rows[row : row + 1, :], in_=bias_dram[row].unsqueeze(0))
+
+        R_COLS = GATES * H_HALVES * P
+        small_t = keep.tile([P, H_HALVES, R_COLS + P], BF16, name="small_t")
+        c0_t = keep.tile([P, H_HALVES, B], F32, name="c0_t")
+        for kh in range(H_HALVES):
+            k_cols = slice(kh * P, (kh + 1) * P)
+            flipped = psum.tile([P, R_COLS + 2 * P], BF16, name="flipped", tag="xt")
+            nc.tensor.transpose(flipped[:, R_COLS : R_COLS + P], h0_sb[:, k_cols], ident_bf16[:])
+            nc.tensor.transpose(flipped[:, R_COLS + P : R_COLS + 2 * P], c0_sb[:, k_cols], ident_bf16[:])
+            for n in range(GATES):
+                for jh in range(H_HALVES):
+                    first = (n * H_HALVES + jh) * P
+                    nc.tensor.transpose(flipped[:, first : first + P], r_sb[:, n, jh, k_cols], ident_bf16[:])
+            nc.vector.tensor_copy(out=small_t[:, kh, :], in_=flipped[:, 0 : R_COLS + P])
+            nc.vector.tensor_copy(out=c0_t[:, kh, :], in_=flipped[:, R_COLS + P : R_COLS + 2 * P])
+
+        w_codes = keep.tile([P, H_HALVES, GATES, PASSES * P], U32, name="w_codes", align_bytes=64)
+        w_scales = keep.tile([P, H_HALVES, GATES, PASSES * P], U8, name="w_scales", align_bytes=64)
+
+        def quantise_w(jh, n):
+            grouped_w = stage.tile([P, PASSES * P * PACK], BF16, name="grouped_w", bufs=3, align_bytes=64)
+            block_to_grouped(
+                nc, psum, w_sb[:, jh, n, :].bitcast(F32), ident_f32[:], grouped_w[:], P, 0, on_vector=(n % 2 == 1)
+            )
+            nc.vector.quantize_mx(
+                out=w_codes[:, jh, n, :].bitcast(FP8X4), scales=w_scales[:, jh, n, :], in_=grouped_w[:]
+            )
+
+        rec = keep.tile([P, H_HALVES, GATES, B], F32, name="rec")
+
+        def recurrent_term(jh):
+            rec_ps = psum.tile([P, GATES, B], F32, name="rec_ps", tag="acc")
+            for n in range(GATES):
+                first = (n * H_HALVES + jh) * P
+                for kh in range(H_HALVES):
+                    nc.tensor.matmul(
+                        out=rec_ps[:, n, :],
+                        lhsT=small_t[:, kh, first : first + P],
+                        rhs=small_t[:, kh, R_COLS : R_COLS + P],
+                        start=(kh == 0),
+                        stop=(kh == H_HALVES - 1),
+                    )
+            nc.vector.tensor_copy(out=rec[:, jh, :, :], in_=rec_ps[:])
+
+        bias_col = keep.tile([P, H_HALVES, GATES], F32, name="bias_col")
+
+        def bias_columns():
+            bias_ps = psum.tile([P, H_HALVES, P], BF16, name="bias_ps", tag="xt")
+            for jh in range(H_HALVES):
+                nc.tensor.transpose(bias_ps[:, jh, :], bias_rows[:, jh * P : (jh + 1) * P], ident_bf16[:])
+            nc.vector.tensor_reduce(
+                out=bias_col[:],
+                in_=bias_ps[:, :, 0 : 2 * GATES].rearrange("p h (n two) -> p h n two", two=2),
+                axis=mybir.AxisListType.X,
+                op=ALU.add,
+            )
+
+        grouped_x = {}
+        x_codes = {}
+        x_scales = {}
+
+        def regroup_chunk(k, vector_share):
+            grouped_x[k] = stage.tile([P, PASSES * N * PACK], BF16, name="grouped_x", align_bytes=64)
+            words = x_sb[k][:].bitcast(F32)
+            for t in range(T_CHUNK):
+                block_to_grouped(
+                    nc, psum, words[:, t * WORDS : (t + 1) * WORDS], ident_f32[:], grouped_x[k][:], N, t * B,
+                    on_vector=(t % vector_share == vector_share - 1),
+                )
+
+        def quantise_chunk(k):
+            x_codes[k] = stage.tile([P, PASSES * N], U32, name="x_codes", bufs=3, align_bytes=64)
+            x_scales[k] = stage.tile([P, PASSES * N], U8, name="x_scales", bufs=3, align_bytes=64)
+            nc.vector.quantize_mx(out=x_codes[k][:].bitcast(FP8X4), scales=x_scales[k][:], in_=grouped_x[k][:])
+
+        gates = {}
+        hidden = {}
+
+        def by_step(ap):
+            return ap.rearrange("p (t b) -> p t b", b=B)
+
+        def over_steps(ap):
+            return ap.unsqueeze(1).to_broadcast([P, T_CHUNK, B])
+
+        def pre_activation(u, n):
+            k, jh = divmod(u, H_HALVES)
+            if n == 0:
+                gates[u] = work.tile([P, GATES, N], F32, name="gates", bufs=LAST_LAG + 2)
+            acc = psum.tile([P, N], F32, name="acc", tag="acc")
+            for g in range(PASSES):
+                nc.tensor.matmul_mx(
+                    out=acc[:],
+                    lhsT=w_codes[:, jh, n, g * P : (g + 1) * P].bitcast(FP8X4),
+                    lhsT_scale=w_scales[:, jh, n, g * P : (g + 1) * P],
+                    rhs=x_codes[k][:, g * N : (g + 1) * N].bitcast(FP8X4),
+                    rhs_scale=x_scales[k][:, g * N : (g + 1) * N],
+                    start=(g == 0),
+                    stop=(g == PASSES - 1),
+                )
+            nc.vector.tensor_tensor(
+                out=by_step(gates[u][:, n, :]), in0=by_step(acc[:]), in1=over_steps(rec[:, jh, n, :]), op=ALU.add
+            )
+
+        def activations(u):
+            jh = u % H_HALVES
+            for n in range(GATES):
+                nc.scalar.activation(
+                    out=gates[u][:, n, :], in_=gates[u][:, n, :], func=GATE_FUNC[n], bias=bias_col[:, jh, n : n + 1]
+                )
+                if n == I_GATE:
+                    nc.gpsimd.tensor_tensor(
+                        out=gates[u][:, I_GATE, :], in0=gates[u][:, I_GATE, :], in1=gates[u][:, G_GATE, :], op=ALU.mult
+                    )
+
+        def forget(u):
+            jh = u % H_HALVES
+            nc.vector.tensor_tensor(
+                out=by_step(gates[u][:, F_GATE, :]),
+                in0=by_step(gates[u][:, F_GATE, :]),
+                in1=over_steps(c0_t[:, jh, :]),
+                op=ALU.mult,
+            )
+
+        def cell(u):
+            nc.gpsimd.tensor_tensor(
+                out=gates[u][:, F_GATE, :], in0=gates[u][:, F_GATE, :], in1=gates[u][:, I_GATE, :], op=ALU.add
+            )
+
+        def output(u):
+            k, jh = divmod(u, H_HALVES)
+            hidden[u] = work.tile([P, N], F32, name="hidden")
+            nc.scalar.activation(out=hidden[u][:], in_=gates[u][:, F_GATE, :], func=ACT.Tanh)
+            first = order[k] * N
+            nc.sync.dma_start(out=out_0[jh * P : (jh + 1) * P, first : first + N], in_=hidden[u][:])
+
+        last_sb = keep.tile([P, 2, H], F32, name="last_sb")
+
+        def last_step(u):
+            jh = u % H_HALVES
+            last_cols = slice((T_CHUNK - 1) * B, T_CHUNK * B)
+            last_ps = psum.tile([P, 2, P], F32, name="last_ps", tag="xt")
+            nc.tensor.transpose(last_ps[:, 0, :], hidden[u][:, last_cols], ident_f32[:])
+            nc.tensor.transpose(last_ps[:, 1, :], gates[u][:, F_GATE, last_cols], ident_f32[:])
+            nc.vector.tensor_copy(out=last_sb[:, :, jh * P : (jh + 1) * P], in_=last_ps[:])
+
+        for n in range(GATES):
+            quantise_w(0, n)
+        for jh in range(H_HALVES):
+            recurrent_term(jh)
+        regroup_chunk(0, vector_share=2)
+        quantise_chunk(0)
+        for n in range(GATES):
+            quantise_w(1, n)
+
+        for step in range(UNITS + LAST_LAG + 1):
+            k, jh = divmod(step, H_HALVES)
+            new_unit = step < UNITS
+            next_chunk = new_unit and k + 1 < CHUNKS
+            has_cell_unit = 0 <= step - CELL_LAG < UNITS
+            if new_unit:
+                pre_activation(step, G_GATE)
+            if next_chunk and jh == 1:
+                quantise_chunk(k + 1)
+            if new_unit:
+                pre_activation(step, I_GATE)
+            if has_cell_unit:
+                forget(step - CELL_LAG)
+                cell(step - CELL_LAG)
+            if new_unit:
+                pre_activation(step, F_GATE)
+            if next_chunk and jh == 0:
+                regroup_chunk(k + 1, vector_share=4)
+            if step == 0:
+                bias_columns()
+            if 0 <= step - ACT_LAG < UNITS:
+                activations(step - ACT_LAG)
+            if 0 <= step - OUT_LAG < UNITS:
+                output(step - OUT_LAG)
+            if 0 <= step - LAST_LAG < H_HALVES:
+                last_step(step - LAST_LAG)
+            if step - LAST_LAG == H_HALVES - 1:
+                nc.sync.dma_start(out=out_1, in_=last_sb[:, 0, :])
+                nc.sync.dma_start(out=out_2, in_=last_sb[:, 1, :])

@@ -212,7 +212,7 @@ def tile_lstm_cell_pa_t_kernel(
                     out=gates[u][:, n, :], in_=gates[u][:, n, :], func=GATE_FUNC[n], bias=bias_col[:, jh, n : n + 1]
                 )
                 if n == I_GATE:
-                    nc.gpsimd.tensor_tensor(
+                    nc.vector.tensor_tensor(
                         out=gates[u][:, I_GATE, :], in0=gates[u][:, I_GATE, :], in1=gates[u][:, G_GATE, :], op=ALU.mult
                     )
 
@@ -226,7 +226,7 @@ def tile_lstm_cell_pa_t_kernel(
             )
 
         def cell(u):
-            nc.gpsimd.tensor_tensor(
+            nc.vector.tensor_tensor(
                 out=gates[u][:, F_GATE, :], in0=gates[u][:, F_GATE, :], in1=gates[u][:, I_GATE, :], op=ALU.add
             )
 

@@ -88,20 +88,22 @@ def tile_lstm_cell_pa_t_kernel(
                     in_=x[:, t0 : t0 + 2, :].rearrange("b t k -> b (t k)"),
                 )
 
+        bias_rows = keep.tile([P, H], BF16, name="bias_rows")
+        nc.vector.memset(bias_rows[:], 0.0)
+
         load_w(0)
         load_x(0)
         load_w(1)
-        for k in range(1, CHUNKS):
+        load_x(1)
+        for row in range(2 * GATES):
+            nc.sync.dma_start(out=bias_rows[row : row + 1, :], in_=bias_dram[row].unsqueeze(0))
+        for k in range(2, CHUNKS):
             load_x(k)
 
         ident_bf16 = keep.tile([P, P], BF16, name="ident_bf16")
         make_identity(nc, ident_bf16[:])
         ident_f32 = keep.tile([P, P], F32, name="ident_f32")
         nc.vector.tensor_copy(out=ident_f32[:], in_=ident_bf16[:])
-        bias_rows = keep.tile([P, H], BF16, name="bias_rows")
-        nc.vector.memset(bias_rows[:], 0.0)
-        for row in range(2 * GATES):
-            nc.gpsimd.dma_start(out=bias_rows[row : row + 1, :], in_=bias_dram[row].unsqueeze(0))
 
         R_COLS = GATES * H_HALVES * P
         small_t = keep.tile([P, H_HALVES, R_COLS + P], BF16, name="small_t")
@@ -163,13 +165,13 @@ def tile_lstm_cell_pa_t_kernel(
         x_codes = {}
         x_scales = {}
 
-        def regroup_chunk(k, vector_share):
+        def regroup_chunk(k, share_with_vector):
             grouped_x[k] = stage.tile([P, PASSES * N * PACK], BF16, name="grouped_x", align_bytes=64)
             words = x_sb[k][:].bitcast(F32)
             for t in range(T_CHUNK):
                 block_to_grouped(
                     nc, psum, words[:, t * WORDS : (t + 1) * WORDS], ident_f32[:], grouped_x[k][:], N, t * B,
-                    on_vector=(t % vector_share == vector_share - 1),
+                    on_vector=(share_with_vector and t % 2 == 1),
                 )
 
         def quantise_chunk(k):
@@ -212,7 +214,7 @@ def tile_lstm_cell_pa_t_kernel(
                     out=gates[u][:, n, :], in_=gates[u][:, n, :], func=GATE_FUNC[n], bias=bias_col[:, jh, n : n + 1]
                 )
                 if n == I_GATE:
-                    nc.vector.tensor_tensor(
+                    nc.gpsimd.tensor_tensor(
                         out=gates[u][:, I_GATE, :], in0=gates[u][:, I_GATE, :], in1=gates[u][:, G_GATE, :], op=ALU.mult
                     )
 
@@ -251,7 +253,7 @@ def tile_lstm_cell_pa_t_kernel(
             quantise_w(0, n)
         for jh in range(H_HALVES):
             recurrent_term(jh)
-        regroup_chunk(0, vector_share=2)
+        regroup_chunk(0, share_with_vector=True)
         quantise_chunk(0)
         for n in range(GATES):
             quantise_w(1, n)
@@ -269,11 +271,12 @@ def tile_lstm_cell_pa_t_kernel(
                 pre_activation(step, I_GATE)
             if has_cell_unit:
                 forget(step - CELL_LAG)
-                cell(step - CELL_LAG)
             if new_unit:
                 pre_activation(step, F_GATE)
+            if has_cell_unit:
+                cell(step - CELL_LAG)
             if next_chunk and jh == 0:
-                regroup_chunk(k + 1, vector_share=4)
+                regroup_chunk(k + 1, share_with_vector=False)
             if step == 0:
                 bias_columns()
             if 0 <= step - ACT_LAG < UNITS:

@@ -35,8 +35,8 @@ LAST_LAG = 5
 FLOPS = 2 * B * T * I * GATES * H + 2 * B * H * GATES * H
 
 
-def block_to_grouped(nc, psum, src_words, ident_f32, grouped, cols, first_col, on_vector):
-    planes = psum.tile([P, PLANES, P], F32, name="planes", tag="xt")
+def block_to_grouped(nc, psum_xt, src_words, ident_f32, grouped, cols, first_col, on_vector):
+    planes = psum_xt.tile([P, PLANES, P], F32, name="planes", tag="xt")
     for q in range(PLANES):
         nc.tensor.transpose(planes[:, q, :], src_words[:, q * P : (q + 1) * P], ident_f32)
     grouped_words = grouped.bitcast(F32).rearrange("p (g c u) -> p g c u", g=PASSES, c=cols)
@@ -62,7 +62,9 @@ def tile_lstm_cell_pa_t_kernel(
         keep = ctx.enter_context(tc.tile_pool(name="keep", bufs=1))
         stage = ctx.enter_context(tc.tile_pool(name="stage", bufs=2))
         work = ctx.enter_context(tc.tile_pool(name="work", bufs=4))
-        psum = ctx.enter_context(tc.psum_pool(name="psum", bufs=4))
+        psum_acc = ctx.enter_context(tc.psum_pool(name="psum_acc", bufs=4))
+        psum_xt = ctx.enter_context(tc.psum_pool(name="psum_xt", bufs=3))
+        psum_keep = ctx.enter_context(tc.psum_pool(name="psum_keep", bufs=1))
 
         h0_sb = keep.tile([P, H], BF16, name="h0_sb")
         nc.sync.dma_start(out=h0_sb[:], in_=h0)
@@ -107,18 +109,17 @@ def tile_lstm_cell_pa_t_kernel(
 
         R_COLS = GATES * H_HALVES * P
         small_t = keep.tile([P, H_HALVES, R_COLS + P], BF16, name="small_t")
-        c0_t = keep.tile([P, H_HALVES, B], F32, name="c0_t")
+        c0_t = psum_keep.tile([P, H_HALVES, B], BF16, name="c0_t")
         for kh in range(H_HALVES):
             k_cols = slice(kh * P, (kh + 1) * P)
-            flipped = psum.tile([P, R_COLS + 2 * P], BF16, name="flipped", tag="xt")
+            flipped = psum_xt.tile([P, R_COLS + P], BF16, name="flipped", tag="xt")
             nc.tensor.transpose(flipped[:, R_COLS : R_COLS + P], h0_sb[:, k_cols], ident_bf16[:])
-            nc.tensor.transpose(flipped[:, R_COLS + P : R_COLS + 2 * P], c0_sb[:, k_cols], ident_bf16[:])
+            nc.tensor.transpose(c0_t[:, kh, :], c0_sb[:, k_cols], ident_bf16[:])
             for n in range(GATES):
                 for jh in range(H_HALVES):
                     first = (n * H_HALVES + jh) * P
                     nc.tensor.transpose(flipped[:, first : first + P], r_sb[:, n, jh, k_cols], ident_bf16[:])
-            nc.vector.tensor_copy(out=small_t[:, kh, :], in_=flipped[:, 0 : R_COLS + P])
-            nc.vector.tensor_copy(out=c0_t[:, kh, :], in_=flipped[:, R_COLS + P : R_COLS + 2 * P])
+            nc.vector.tensor_copy(out=small_t[:, kh, :], in_=flipped[:])
 
         w_codes = keep.tile([P, H_HALVES, GATES, PASSES * P], U32, name="w_codes", align_bytes=64)
         w_scales = keep.tile([P, H_HALVES, GATES, PASSES * P], U8, name="w_scales", align_bytes=64)
@@ -126,7 +127,7 @@ def tile_lstm_cell_pa_t_kernel(
         def quantise_w(jh, n):
             grouped_w = stage.tile([P, PASSES * P * PACK], BF16, name="grouped_w", bufs=3, align_bytes=64)
             block_to_grouped(
-                nc, psum, w_sb[:, jh, n, :].bitcast(F32), ident_f32[:], grouped_w[:], P, 0, on_vector=(n % 2 == 1)
+                nc, psum_xt, w_sb[:, jh, n, :].bitcast(F32), ident_f32[:], grouped_w[:], P, 0, on_vector=(n % 2 == 1)
             )
             nc.vector.quantize_mx(
                 out=w_codes[:, jh, n, :].bitcast(FP8X4), scales=w_scales[:, jh, n, :], in_=grouped_w[:]
@@ -135,7 +136,7 @@ def tile_lstm_cell_pa_t_kernel(
         rec = keep.tile([P, H_HALVES, GATES, B], F32, name="rec")
 
         def recurrent_term(jh):
-            rec_ps = psum.tile([P, GATES, B], F32, name="rec_ps", tag="acc")
+            rec_ps = psum_acc.tile([P, GATES, B], F32, name="rec_ps", tag="acc")
             for n in range(GATES):
                 first = (n * H_HALVES + jh) * P
                 for kh in range(H_HALVES):
@@ -151,7 +152,7 @@ def tile_lstm_cell_pa_t_kernel(
         bias_col = keep.tile([P, H_HALVES, GATES], F32, name="bias_col")
 
         def bias_columns():
-            bias_ps = psum.tile([P, H_HALVES, P], BF16, name="bias_ps", tag="xt")
+            bias_ps = psum_xt.tile([P, H_HALVES, P], BF16, name="bias_ps", tag="xt")
             for jh in range(H_HALVES):
                 nc.tensor.transpose(bias_ps[:, jh, :], bias_rows[:, jh * P : (jh + 1) * P], ident_bf16[:])
             nc.vector.tensor_reduce(
@@ -170,7 +171,7 @@ def tile_lstm_cell_pa_t_kernel(
             words = x_sb[k][:].bitcast(F32)
             for t in range(T_CHUNK):
                 block_to_grouped(
-                    nc, psum, words[:, t * WORDS : (t + 1) * WORDS], ident_f32[:], grouped_x[k][:], N, t * B,
+                    nc, psum_xt, words[:, t * WORDS : (t + 1) * WORDS], ident_f32[:], grouped_x[k][:], N, t * B,
                     on_vector=(share_with_vector and t % 2 == 1),
                 )
 
@@ -192,7 +193,7 @@ def tile_lstm_cell_pa_t_kernel(
             k, jh = divmod(u, H_HALVES)
             if n == 0:
                 gates[u] = work.tile([P, GATES, N], F32, name="gates", bufs=LAST_LAG + 2)
-            acc = psum.tile([P, N], F32, name="acc", tag="acc")
+            acc = psum_acc.tile([P, N], F32, name="acc", tag="acc")
             for g in range(PASSES):
                 nc.tensor.matmul_mx(
                     out=acc[:],
@@ -228,7 +229,7 @@ def tile_lstm_cell_pa_t_kernel(
             )
 
         def cell(u):
-            nc.vector.tensor_tensor(
+            nc.gpsimd.tensor_tensor(
                 out=gates[u][:, F_GATE, :], in0=gates[u][:, F_GATE, :], in1=gates[u][:, I_GATE, :], op=ALU.add
             )
 
@@ -244,7 +245,7 @@ def tile_lstm_cell_pa_t_kernel(
         def last_step(u):
             jh = u % H_HALVES
             last_cols = slice((T_CHUNK - 1) * B, T_CHUNK * B)
-            last_ps = psum.tile([P, 2, P], F32, name="last_ps", tag="xt")
+            last_ps = psum_xt.tile([P, 2, P], F32, name="last_ps", tag="xt")
             nc.tensor.transpose(last_ps[:, 0, :], hidden[u][:, last_cols], ident_f32[:])
             nc.tensor.transpose(last_ps[:, 1, :], gates[u][:, F_GATE, last_cols], ident_f32[:])
             nc.vector.tensor_copy(out=last_sb[:, :, jh * P : (jh + 1) * P], in_=last_ps[:])
@@ -271,10 +272,9 @@ def tile_lstm_cell_pa_t_kernel(
                 pre_activation(step, I_GATE)
             if has_cell_unit:
                 forget(step - CELL_LAG)
+                cell(step - CELL_LAG)
             if new_unit:
                 pre_activation(step, F_GATE)
-            if has_cell_unit:
-                cell(step - CELL_LAG)
             if next_chunk and jh == 0:
                 regroup_chunk(k + 1, share_with_vector=False)
             if step == 0:

@@ -58,7 +58,6 @@ def tile_lstm_cell_pa_t_kernel(
     order = list(reversed(range(CHUNKS)))
 
     with ExitStack() as ctx:
-        ctx.enter_context(tc.manual_schedule())
         keep = ctx.enter_context(tc.tile_pool(name="keep", bufs=1))
         stage = ctx.enter_context(tc.tile_pool(name="stage", bufs=2))
         work = ctx.enter_context(tc.tile_pool(name="work", bufs=4))

@@ -31,6 +31,7 @@ ACT_LAG = 1
 CELL_LAG = 2
 OUT_LAG = 3
 LAST_LAG = 5
+TAIL_UNITS = 2
 
 FLOPS = 2 * B * T * I * GATES * H + 2 * B * H * GATES * H
 
@@ -64,6 +65,10 @@ def tile_lstm_cell_pa_t_kernel(
         psum_acc = ctx.enter_context(tc.psum_pool(name="psum_acc", bufs=4))
         psum_xt = ctx.enter_context(tc.psum_pool(name="psum_xt", bufs=3))
         psum_keep = ctx.enter_context(tc.psum_pool(name="psum_keep", bufs=1))
+
+        warm = keep.tile([P, 1], F32, name="warm")
+        nc.vector.memset(warm[:], 0.0)
+        nc.scalar.activation(out=warm[:], in_=warm[:], func=ACT.Sigmoid)
 
         h0_sb = keep.tile([P, H], BF16, name="h0_sb")
         nc.sync.dma_start(out=h0_sb[:], in_=h0)
@@ -207,6 +212,9 @@ def tile_lstm_cell_pa_t_kernel(
                 out=by_step(gates[u][:, n, :]), in0=by_step(acc[:]), in1=over_steps(rec[:, jh, n, :]), op=ALU.add
             )
 
+        def elementwise_engine(u):
+            return nc.vector if u >= UNITS - TAIL_UNITS else nc.gpsimd
+
         def activations(u):
             jh = u % H_HALVES
             for n in range(GATES):
@@ -214,7 +222,7 @@ def tile_lstm_cell_pa_t_kernel(
                     out=gates[u][:, n, :], in_=gates[u][:, n, :], func=GATE_FUNC[n], bias=bias_col[:, jh, n : n + 1]
                 )
                 if n == I_GATE:
-                    nc.gpsimd.tensor_tensor(
+                    elementwise_engine(u).tensor_tensor(
                         out=gates[u][:, I_GATE, :], in0=gates[u][:, I_GATE, :], in1=gates[u][:, G_GATE, :], op=ALU.mult
                     )
 
@@ -228,7 +236,7 @@ def tile_lstm_cell_pa_t_kernel(
             )
 
         def cell(u):
-            nc.gpsimd.tensor_tensor(
+            elementwise_engine(u).tensor_tensor(
                 out=gates[u][:, F_GATE, :], in0=gates[u][:, F_GATE, :], in1=gates[u][:, I_GATE, :], op=ALU.add
             )
 

from contextlib import ExitStack

import concourse.mybir as mybir
from concourse.masks import make_identity

F32 = mybir.dt.float32
BF16 = mybir.dt.bfloat16
U32 = mybir.dt.uint32
U8 = mybir.dt.uint8
FP8X4 = mybir.dt.float8_e4m3fn_x4
ACT = mybir.ActivationFunctionType
ALU = mybir.AluOpType

P = 128
B, T, I, H = 128, 32, 1024, 256
GATES = 3
G_GATE, I_GATE, F_GATE = 0, 1, 2
GATE_FUNC = (ACT.Tanh, ACT.Sigmoid, ACT.Sigmoid)
PACK = 4
K_PASS = P * PACK
PASSES = I // K_PASS
WORDS = I // 2
PLANES = WORDS // P
H_HALVES = H // P
T_CHUNK = 4
N = T_CHUNK * B
CHUNKS = T // T_CHUNK
UNITS = CHUNKS * H_HALVES

ACT_LAG = 1
CELL_LAG = 2
OUT_LAG = 3
LAST_LAG = 5
TAIL_UNITS = 2

FLOPS = 2 * B * T * I * GATES * H + 2 * B * H * GATES * H


def block_to_grouped(nc, psum_xt, src_words, ident_f32, grouped, cols, first_col, on_vector):
    planes = psum_xt.tile([P, PLANES, P], F32, name="planes", tag="xt")
    for q in range(PLANES):
        nc.tensor.transpose(planes[:, q, :], src_words[:, q * P : (q + 1) * P], ident_f32)
    grouped_words = grouped.bitcast(F32).rearrange("p (g c u) -> p g c u", g=PASSES, c=cols)
    dst = grouped_words[:, :, first_col : first_col + P, :]
    src = planes[:].rearrange("p (g u) c -> p g c u", g=PASSES)
    if on_vector:
        nc.vector.tensor_copy(out=dst, in_=src)
    else:
        nc.scalar.copy(out=dst, in_=src)


def tile_lstm_cell_pa_t_kernel(
    tc, x, h0, c0, W_f, b_f, R_f, rb_f, W_i, b_i, R_i, rb_i, W_g, b_g, R_g, rb_g, out_0, out_1, out_2
):
    nc = tc.nc
    w_dram = (W_g, W_i, W_f)
    r_dram = (R_g, R_i, R_f)
    bias_dram = (b_g, rb_g, b_i, rb_i, b_f, rb_f)
    order = list(reversed(range(CHUNKS)))

    with ExitStack() as ctx:
        keep = ctx.enter_context(tc.tile_pool(name="keep", bufs=1))
        stage = ctx.enter_context(tc.tile_pool(name="stage", bufs=2))
        work = ctx.enter_context(tc.tile_pool(name="work", bufs=4))
        psum_acc = ctx.enter_context(tc.psum_pool(name="psum_acc", bufs=4))
        psum_xt = ctx.enter_context(tc.psum_pool(name="psum_xt", bufs=3))
        psum_keep = ctx.enter_context(tc.psum_pool(name="psum_keep", bufs=1))

        warm = keep.tile([P, 1], F32, name="warm")
        nc.vector.memset(warm[:], 0.0)
        nc.scalar.activation(out=warm[:], in_=warm[:], func=ACT.Sigmoid)

        h0_sb = keep.tile([P, H], BF16, name="h0_sb")
        nc.sync.dma_start(out=h0_sb[:], in_=h0)
        c0_sb = keep.tile([P, H], BF16, name="c0_sb")
        nc.sync.dma_start(out=c0_sb[:], in_=c0)
        r_sb = keep.tile([P, GATES, H_HALVES, H], BF16, name="r_sb")
        for n in range(GATES):
            nc.sync.dma_start(out=r_sb[:, n, :, :], in_=r_dram[n].rearrange("(h j) k -> j h k", j=P))
        w_sb = keep.tile([P, H_HALVES, GATES, I], BF16, name="w_sb")
        x_sb = []
        for k in range(CHUNKS):
            x_sb.append(keep.tile([P, T_CHUNK * I], BF16, name="x_sb%d" % k))

        def load_w(jh):
            for n in range(GATES):
                nc.sync.dma_start(out=w_sb[:, jh, n, :], in_=w_dram[n][jh * P : (jh + 1) * P, :])

        def load_x(k):
            for half in range(2):
                t0 = order[k] * T_CHUNK + half * 2
                nc.sync.dma_start(
                    out=x_sb[k][:, half * 2 * I : (half + 1) * 2 * I],
                    in_=x[:, t0 : t0 + 2, :].rearrange("b t k -> b (t k)"),
                )

        bias_rows = keep.tile([P, H], BF16, name="bias_rows")
        nc.vector.memset(bias_rows[:], 0.0)

        load_w(0)
        load_x(0)
        load_w(1)
        load_x(1)
        for row in range(2 * GATES):
            nc.sync.dma_start(out=bias_rows[row : row + 1, :], in_=bias_dram[row].unsqueeze(0))
        for k in range(2, CHUNKS):
            load_x(k)

        ident_bf16 = keep.tile([P, P], BF16, name="ident_bf16")
        make_identity(nc, ident_bf16[:])
        ident_f32 = keep.tile([P, P], F32, name="ident_f32")
        nc.vector.tensor_copy(out=ident_f32[:], in_=ident_bf16[:])

        R_COLS = GATES * H_HALVES * P
        small_t = keep.tile([P, H_HALVES, R_COLS + P], BF16, name="small_t")
        c0_t = psum_keep.tile([P, H_HALVES, B], BF16, name="c0_t")
        for kh in range(H_HALVES):
            k_cols = slice(kh * P, (kh + 1) * P)
            flipped = psum_xt.tile([P, R_COLS + P], BF16, name="flipped", tag="xt")
            nc.tensor.transpose(flipped[:, R_COLS : R_COLS + P], h0_sb[:, k_cols], ident_bf16[:])
            nc.tensor.transpose(c0_t[:, kh, :], c0_sb[:, k_cols], ident_bf16[:])
            for n in range(GATES):
                for jh in range(H_HALVES):
                    first = (n * H_HALVES + jh) * P
                    nc.tensor.transpose(flipped[:, first : first + P], r_sb[:, n, jh, k_cols], ident_bf16[:])
            nc.vector.tensor_copy(out=small_t[:, kh, :], in_=flipped[:])

        w_codes = keep.tile([P, H_HALVES, GATES, PASSES * P], U32, name="w_codes", align_bytes=64)
        w_scales = keep.tile([P, H_HALVES, GATES, PASSES * P], U8, name="w_scales", align_bytes=64)

        def quantise_w(jh, n):
            grouped_w = stage.tile([P, PASSES * P * PACK], BF16, name="grouped_w", bufs=3, align_bytes=64)
            block_to_grouped(
                nc, psum_xt, w_sb[:, jh, n, :].bitcast(F32), ident_f32[:], grouped_w[:], P, 0, on_vector=(n % 2 == 1)
            )
            nc.vector.quantize_mx(
                out=w_codes[:, jh, n, :].bitcast(FP8X4), scales=w_scales[:, jh, n, :], in_=grouped_w[:]
            )

        rec = keep.tile([P, H_HALVES, GATES, B], F32, name="rec")

        def recurrent_term(jh):
            rec_ps = psum_acc.tile([P, GATES, B], F32, name="rec_ps", tag="acc")
            for n in range(GATES):
                first = (n * H_HALVES + jh) * P
                for kh in range(H_HALVES):
                    nc.tensor.matmul(
                        out=rec_ps[:, n, :],
                        lhsT=small_t[:, kh, first : first + P],
                        rhs=small_t[:, kh, R_COLS : R_COLS + P],
                        start=(kh == 0),
                        stop=(kh == H_HALVES - 1),
                    )
            nc.vector.tensor_copy(out=rec[:, jh, :, :], in_=rec_ps[:])

        bias_col = keep.tile([P, H_HALVES, GATES], F32, name="bias_col")

        def bias_columns():
            bias_ps = psum_xt.tile([P, H_HALVES, P], BF16, name="bias_ps", tag="xt")
            for jh in range(H_HALVES):
                nc.tensor.transpose(bias_ps[:, jh, :], bias_rows[:, jh * P : (jh + 1) * P], ident_bf16[:])
            nc.vector.tensor_reduce(
                out=bias_col[:],
                in_=bias_ps[:, :, 0 : 2 * GATES].rearrange("p h (n two) -> p h n two", two=2),
                axis=mybir.AxisListType.X,
                op=ALU.add,
            )

        grouped_x = {}
        x_codes = {}
        x_scales = {}

        def regroup_chunk(k, share_with_vector):
            grouped_x[k] = stage.tile([P, PASSES * N * PACK], BF16, name="grouped_x", align_bytes=64)
            words = x_sb[k][:].bitcast(F32)
            for t in range(T_CHUNK):
                block_to_grouped(
                    nc, psum_xt, words[:, t * WORDS : (t + 1) * WORDS], ident_f32[:], grouped_x[k][:], N, t * B,
                    on_vector=(share_with_vector and t % 2 == 1),
                )

        def quantise_chunk(k):
            x_codes[k] = stage.tile([P, PASSES * N], U32, name="x_codes", bufs=3, align_bytes=64)
            x_scales[k] = stage.tile([P, PASSES * N], U8, name="x_scales", bufs=3, align_bytes=64)
            nc.vector.quantize_mx(out=x_codes[k][:].bitcast(FP8X4), scales=x_scales[k][:], in_=grouped_x[k][:])

        gates = {}
        hidden = {}

        def by_step(ap):
            return ap.rearrange("p (t b) -> p t b", b=B)

        def over_steps(ap):
            return ap.unsqueeze(1).to_broadcast([P, T_CHUNK, B])

        def pre_activation(u, n):
            k, jh = divmod(u, H_HALVES)
            if n == 0:
                gates[u] = work.tile([P, GATES, N], F32, name="gates", bufs=LAST_LAG + 2)
            acc = psum_acc.tile([P, N], F32, name="acc", tag="acc")
            for g in range(PASSES):
                nc.tensor.matmul_mx(
                    out=acc[:],
                    lhsT=w_codes[:, jh, n, g * P : (g + 1) * P].bitcast(FP8X4),
                    lhsT_scale=w_scales[:, jh, n, g * P : (g + 1) * P],
                    rhs=x_codes[k][:, g * N : (g + 1) * N].bitcast(FP8X4),
                    rhs_scale=x_scales[k][:, g * N : (g + 1) * N],
                    start=(g == 0),
                    stop=(g == PASSES - 1),
                )
            nc.vector.tensor_tensor(
                out=by_step(gates[u][:, n, :]), in0=by_step(acc[:]), in1=over_steps(rec[:, jh, n, :]), op=ALU.add
            )

        def elementwise_engine(u):
            return nc.vector if u >= UNITS - TAIL_UNITS else nc.gpsimd

        def activations(u):
            jh = u % H_HALVES
            for n in range(GATES):
                nc.scalar.activation(
                    out=gates[u][:, n, :], in_=gates[u][:, n, :], func=GATE_FUNC[n], bias=bias_col[:, jh, n : n + 1]
                )
                if n == I_GATE:
                    elementwise_engine(u).tensor_tensor(
                        out=gates[u][:, I_GATE, :], in0=gates[u][:, I_GATE, :], in1=gates[u][:, G_GATE, :], op=ALU.mult
                    )

        def forget(u):
            jh = u % H_HALVES
            nc.vector.tensor_tensor(
                out=by_step(gates[u][:, F_GATE, :]),
                in0=by_step(gates[u][:, F_GATE, :]),
                in1=over_steps(c0_t[:, jh, :]),
                op=ALU.mult,
            )

        def cell(u):
            elementwise_engine(u).tensor_tensor(
                out=gates[u][:, F_GATE, :], in0=gates[u][:, F_GATE, :], in1=gates[u][:, I_GATE, :], op=ALU.add
            )

        def output(u):
            k, jh = divmod(u, H_HALVES)
            hidden[u] = work.tile([P, N], F32, name="hidden")
            nc.scalar.activation(out=hidden[u][:], in_=gates[u][:, F_GATE, :], func=ACT.Tanh)
            first = order[k] * N
            nc.sync.dma_start(out=out_0[jh * P : (jh + 1) * P, first : first + N], in_=hidden[u][:])

        last_sb = keep.tile([P, 2, H], F32, name="last_sb")

        def last_step(u):
            jh = u % H_HALVES
            last_cols = slice((T_CHUNK - 1) * B, T_CHUNK * B)
            last_ps = psum_xt.tile([P, 2, P], F32, name="last_ps", tag="xt")
            nc.tensor.transpose(last_ps[:, 0, :], hidden[u][:, last_cols], ident_f32[:])
            nc.tensor.transpose(last_ps[:, 1, :], gates[u][:, F_GATE, last_cols], ident_f32[:])
            nc.vector.tensor_copy(out=last_sb[:, :, jh * P : (jh + 1) * P], in_=last_ps[:])

        for n in range(GATES):
            quantise_w(0, n)
        for jh in range(H_HALVES):
            recurrent_term(jh)
        regroup_chunk(0, share_with_vector=True)
        quantise_chunk(0)
        for n in range(GATES):
            quantise_w(1, n)

        for step in range(UNITS + LAST_LAG + 1):
            k, jh = divmod(step, H_HALVES)
            new_unit = step < UNITS
            next_chunk = new_unit and k + 1 < CHUNKS
            has_cell_unit = 0 <= step - CELL_LAG < UNITS
            if new_unit:
                pre_activation(step, G_GATE)
            if next_chunk and jh == 1:
                quantise_chunk(k + 1)
            if new_unit:
                pre_activation(step, I_GATE)
            if has_cell_unit:
                forget(step - CELL_LAG)
                cell(step - CELL_LAG)
            if new_unit:
                pre_activation(step, F_GATE)
            if next_chunk and jh == 0:
                regroup_chunk(k + 1, share_with_vector=False)
            if step == 0:
                bias_columns()
            if 0 <= step - ACT_LAG < UNITS:
                activations(step - ACT_LAG)
            if 0 <= step - OUT_LAG < UNITS:
                output(step - OUT_LAG)
            if 0 <= step - LAST_LAG < H_HALVES:
                last_step(step - LAST_LAG)
            if step - LAST_LAG == H_HALVES - 1:
                nc.sync.dma_start(out=out_1, in_=last_sb[:, 0, :])
                nc.sync.dma_start(out=out_2, in_=last_sb[:, 1, :])
